import numpy as np
import ml_dtypes


BF16 = ml_dtypes.bfloat16


def bf(x):
    return np.asarray(x, np.float32).astype(BF16)


def f64(x):
    return np.asarray(x).astype(np.float64)


E2M1 = np.array([0.0, 0.5, 1.0, 1.5, 2.0, 3.0, 4.0, 6.0, -0.0, -0.5, -1.0, -1.5, -2.0, -3.0, -4.0, -6.0])


def pack_weight(w, fmt):
    k, n = w.shape
    w = f64(bf(w)).reshape(k // 32, 32, n)
    amax = np.abs(w).max(1)
    if fmt == "e4m3":
        byte = np.frexp(amax)[1] - 1 + 127 - 7
    else:
        mant, ex = np.frexp(amax / 6.0)
        byte = np.where(mant > 0.5, ex, ex - 1) + 127
    byte = np.clip(np.where(amax > 0, byte, 1), 1, 254)
    scaled = (w * np.exp2(127.0 - byte)[:, None, :]).reshape(k, n).astype(np.float32)
    by_word = np.ascontiguousarray(scaled.reshape(k // 512, 128, 4, n).transpose(0, 1, 3, 2))
    if fmt == "e4m3":
        words = by_word.astype(ml_dtypes.float8_e4m3fn).view(np.uint8)
    else:
        c = by_word.astype(ml_dtypes.float4_e2m1fn).view(np.uint8) & 0xF
        words = c[..., 0::2] | (c[..., 1::2] << 4)
    return np.ascontiguousarray(words), np.ascontiguousarray(byte.astype(np.uint8).reshape(k // 512, 16, n))


def unpack_weight(words, scales, fmt):
    g, p, n, _ = words.shape
    if fmt == "e4m3":
        vals = np.ascontiguousarray(words).view(ml_dtypes.float8_e4m3fn).astype(np.float64)
    else:
        nib = np.empty((g, p, n, 4), np.uint8)
        nib[..., 0::2] = words & 0xF
        nib[..., 1::2] = words >> 4
        vals = E2M1[nib]
    vals = vals * np.repeat(np.exp2(scales.astype(np.float64) - 127.0), 8, axis=1)[..., None]
    return vals.transpose(0, 1, 3, 2).reshape(g * 512, n)

def pack4(w):
    words, scales = pack_weight(w, "e2m1")
    return words.reshape(words.shape[0], 128, -1), scales


def unpack4(words, scales):
    return unpack_weight(words.reshape(words.shape[0], 128, -1, 2), scales, "e2m1")


def kspread(k):
    return np.exp2(np.repeat(np.random.randint(-6, 7, k // 32), 32).astype(np.float64))


B, S, H, NH, FF = 2, 512, 1024, 8, 4096
EPS = 1e-7


def layer_norm(x, g, b):
    m = x.mean(-1, keepdims=True)
    v = ((x - m) ** 2).mean(-1, keepdims=True)
    return (x - m) / np.sqrt(v + EPS) * g + b


def setup_inputs():
    s = kspread(FF)
    r = np.random.standard_normal
    ff = r((B, S, FF)) * 0.65 * s
    ff_words, ff_scales = pack4(ff.reshape(B * S, FF).T)
    attn_out = bf(r((B, S, H)))
    Wf_words, Wf_scales = pack4(r((FF, H)) * 1.5 / np.sqrt(FF) / s[:, None])
    return {"ff_words": ff_words, "ff_scales": ff_scales, "attn_out": attn_out,
            "Wf_words": Wf_words, "Wf_scales": Wf_scales, "b_f": bf(r(H) * 0.2),
            "ln2_g": bf(1.0 + 0.1 * r(H)), "ln2_b": bf(0.1 * r(H))}


def reference(ff_words, ff_scales, attn_out, Wf_words, Wf_scales, b_f, ln2_g, ln2_b):
    ff = unpack4(ff_words, ff_scales).T.reshape(B, S, FF)
    u = (ff @ unpack4(Wf_words, Wf_scales)) + f64(b_f) + f64(attn_out)
    return layer_norm(u, f64(ln2_g), f64(ln2_b))

@@ -1,0 +1,356 @@
+from contextlib import ExitStack
+
+import concourse.mybir as mybir
+
+FLOPS = 2 * 1024 * 4096 * 1024
+
+F32 = mybir.dt.float32
+BF16 = mybir.dt.bfloat16
+I32 = mybir.dt.int32
+U8 = mybir.dt.uint8
+FP4 = mybir.dt.float4_e2m1fn_x4
+ALU = mybir.AluOpType
+ACT = mybir.ActivationFunctionType
+
+P = 128
+H = 1024
+HALF = 512
+NPASS = 8
+NT = 8
+EPS = 1e-7
+TH = 512
+NHEAD = 3
+RUNS = ((0,), (1, 2, 3), (4, 5, 6, 7))
+FA_GROUPS = ((0,), (1, 2, 3), (4, 5, 6, 7))
+FB_GROUPS = ((4, 5), (6, 7))
+VC = 512
+VC_LAST = 768
+
+
+def tile_disentangledattention_pc_kernel(
+    tc, ff_words, ff_scales, attn_out, Wf_words, Wf_scales, b_f, ln2_g, ln2_b, out
+):
+    nc = tc.nc
+    attn = attn_out.flatten_outer_dims()
+    outf = out.flatten_outer_dims()
+
+    with ExitStack() as ctx:
+        const = ctx.enter_context(tc.tile_pool(name="const", bufs=1))
+        codes = ctx.enter_context(tc.tile_pool(name="codes", bufs=1))
+        planes = ctx.enter_context(tc.tile_pool(name="planes", bufs=1))
+        res = ctx.enter_context(tc.tile_pool(name="res", bufs=1))
+        work = ctx.enter_context(tc.tile_pool(name="work", bufs=3))
+        stats = ctx.enter_context(tc.tile_pool(name="stats", bufs=1))
+        psum = ctx.enter_context(tc.psum_pool(name="psum", bufs=1))
+        ctx.enter_context(tc.manual_schedule())
+
+        wpl = []
+        fpl = []
+        for i, run in enumerate(RUNS):
+            wpl_i = planes.tile([P, len(run), H], U8, name="wpl%d" % i, tag="wpl%d" % i, align_bytes=64)
+            fpl_i = planes.tile([P, len(run), TH], U8, name="fpl%d" % i, tag="fpl%d" % i, align_bytes=64)
+            wpl.append(wpl_i)
+            fpl.append(fpl_i)
+        fplb = planes.tile([P, NPASS, H - TH], U8, name="fplb", tag="fplb", align_bytes=64)
+        wc = []
+        for g in range(NPASS):
+            wc_g = codes.tile([P, 2 * H], U8, name="wc%d" % g, tag="wc%d" % g, align_bytes=64)
+            wc.append(wc_g)
+        fa = []
+        for i, grp in enumerate(FA_GROUPS):
+            fa_i = codes.tile([P, len(grp), 2 * TH], U8, name="fa%d" % i, tag="fa%d" % i, align_bytes=64)
+            fa.append(fa_i)
+        fb = []
+        for i, grp in enumerate(FB_GROUPS):
+            fb_i = codes.tile([P, NPASS, 256 * len(grp)], U8, name="fb%d" % i, tag="fb%d" % i, align_bytes=64)
+            fb.append(fb_i)
+        run_of = {}
+        for i, run in enumerate(RUNS):
+            for j, g in enumerate(run):
+                run_of[g] = (i, j)
+        fa_of = {}
+        for i, grp in enumerate(FA_GROUPS):
+            for j, g in enumerate(grp):
+                fa_of[g] = (i, j)
+        fb_of = {}
+        for i, grp in enumerate(FB_GROUPS):
+            for j, t in enumerate(grp):
+                fb_of[t] = (i, j)
+
+        ones = const.tile([P, P], BF16, name="ones", tag="ones")
+        zrow = {}
+        for nm in ("bf", "g", "b"):
+            z_nm = const.tile([P, H], BF16, name="z_%s" % nm, tag="z_%s" % nm)
+            zrow[nm] = z_nm
+        bf_sb = const.tile([P, H], BF16, name="bf_sb", tag="bf_sb")
+        b_sb = const.tile([P, H], BF16, name="b_sb", tag="b_sb")
+        eps_t = const.tile([P, 1], F32, name="eps_t", tag="eps_t")
+        warm = const.tile([P, 1], F32, name="warm", tag="warm")
+        g_ps = psum.tile([P, H], BF16, name="g_ps", tag="g_ps")
+        b_ps = psum.tile([P, H], BF16, name="b_ps", tag="b_ps")
+
+        at = []
+        for t in range(NT):
+            at_t = res.tile([P, H], BF16, name="at%d" % t, tag="at%d" % t)
+            at.append(at_t)
+        resid = []
+        for t in range(NT):
+            r_t = res.tile([P, H], F32, name="resid%d" % t, tag="resid%d" % t)
+            resid.append(r_t)
+
+        nc.vector.memset(wpl[0][:].bitcast(I32), 0)
+        nc.vector.memset(fpl[0][:].bitcast(I32), 0)
+        nc.vector.memset(ones[:], 1.0)
+        nc.vector.memset(eps_t[:], EPS)
+        for nm, vec in (("bf", b_f), ("g", ln2_g), ("b", ln2_b)):
+            nc.gpsimd.memset(zrow[nm][:].bitcast(F32), 0.0)
+            nc.scalar.dma_start(out=zrow[nm][0:1, :], in_=vec.unsqueeze(0))
+        nc.scalar.activation(out=warm[:], in_=eps_t[:], func=ACT.Sqrt)
+        for i in range(1, len(RUNS)):
+            nc.vector.memset(wpl[i][:].bitcast(I32), 0)
+            nc.vector.memset(fpl[i][:].bitcast(I32), 0)
+        nc.vector.memset(fplb[:].bitcast(I32), 0)
+
+
+        def load_scale_run(i):
+            g0 = RUNS[i][0]
+            g1 = RUNS[i][-1] + 1
+            for q in range(4):
+                nc.sync.dma_start(
+                    out=wpl[i][32 * q : 32 * q + 4, :, :].bitcast(I32),
+                    in_=Wf_scales[g0:g1, 4 * q : 4 * q + 4, :].rearrange("g r n -> r g n").bitcast(I32),
+                )
+            for q in range(4):
+                nc.sync.dma_start(
+                    out=fpl[i][32 * q : 32 * q + 4, :, :].bitcast(I32),
+                    in_=ff_scales[g0:g1, 4 * q : 4 * q + 4, 0:TH].rearrange("g r n -> r g n").bitcast(I32),
+                )
+
+        def load_w(g):
+            nc.sync.dma_start(out=wc[g][:].bitcast(I32), in_=Wf_words[g].bitcast(I32))
+
+        def load_fa(i):
+            g0 = FA_GROUPS[i][0]
+            g1 = FA_GROUPS[i][-1] + 1
+            nc.sync.dma_start(
+                out=fa[i][:].bitcast(I32),
+                in_=ff_words[g0:g1, :, 0 : 2 * TH].rearrange("g p n -> p g n").bitcast(I32),
+            )
+
+        def load_fb(i):
+            t0 = FB_GROUPS[i][0]
+            t1 = FB_GROUPS[i][-1] + 1
+            nc.sync.dma_start(
+                out=fb[i][:].bitcast(I32),
+                in_=ff_words[:, :, 256 * t0 : 256 * t1].rearrange("g p n -> p g n").bitcast(I32),
+            )
+
+        def load_fplb():
+            for q in range(4):
+                nc.sync.dma_start(
+                    out=fplb[32 * q : 32 * q + 4, :, :].bitcast(I32),
+                    in_=ff_scales[:, 4 * q : 4 * q + 4, TH:H].rearrange("g r n -> r g n").bitcast(I32),
+                )
+
+        def load_at(t):
+            nc.sync.dma_start(out=at[t][:], in_=attn[P * t : P * (t + 1), :])
+
+        load_w(0)
+        load_fa(0)
+        load_scale_run(0)
+        load_w(1)
+        load_fa(1)
+        load_scale_run(1)
+        load_w(2)
+        load_w(3)
+        load_w(4)
+        load_fa(2)
+        load_scale_run(2)
+        load_w(5)
+        load_w(6)
+        load_w(7)
+        load_at(0)
+        load_at(1)
+        load_fplb()
+        load_fb(0)
+        load_at(2)
+        load_at(3)
+        load_fb(1)
+        load_at(4)
+        load_at(5)
+        load_at(6)
+        load_at(7)
+
+        def broadcast(nm, dst):
+            for h in range(2):
+                nc.tensor.matmul(
+                    out=dst[:, HALF * h : HALF * (h + 1)],
+                    lhsT=ones[:],
+                    rhs=zrow[nm][:, HALF * h : HALF * (h + 1)],
+                    start=True,
+                    stop=True,
+                )
+
+
+        acc = {}
+
+        def open_bank(t, k, bank):
+            a_tk = psum.tile([P, HALF], F32, name="acc%d_%d" % (t, k), tag="bank%d" % bank)
+            acc[(t, k)] = a_tk
+
+        def open_banks(t):
+            for h in range(2):
+                open_bank(t, h, 2 * (t % 3) + h)
+
+        def mx(t, g, k, c0=None, c1=None):
+            if c0 is None:
+                c0 = HALF * k
+                c1 = HALF * (k + 1)
+            if P * t < TH:
+                i, j = fa_of[g]
+                lhs = fa[i][:, j, 256 * t : 256 * (t + 1)]
+                i, j = run_of[g]
+                lhs_s = fpl[i][:, j, P * t : P * (t + 1)]
+            else:
+                i, j = fb_of[t]
+                lhs = fb[i][:, g, 256 * j : 256 * (j + 1)]
+                lhs_s = fplb[:, g, P * t - TH : P * (t + 1) - TH]
+            i, j = run_of[g]
+            nc.tensor.matmul_mx(
+                out=acc[(t, k)][:, 0 : c1 - c0],
+                lhsT=lhs.bitcast(FP4),
+                lhsT_scale=lhs_s,
+                rhs=wc[g][:, 2 * c0 : 2 * c1].bitcast(FP4),
+                rhs_scale=wpl[i][:, j, c0:c1],
+                start=(g == 0),
+                stop=(g == NPASS - 1),
+            )
+
+        bf_ps = psum.tile([P, H], BF16, name="bf_ps", tag="bank5")
+        broadcast("bf", bf_ps)
+        nc.scalar.copy(out=bf_sb[:], in_=bf_ps[:])
+        broadcast("g", g_ps)
+        broadcast("b", b_ps)
+        nc.scalar.copy(out=b_sb[:], in_=b_ps[:])
+        for t in range(NHEAD):
+            open_banks(t)
+        for g in range(NPASS):
+            for t in range(NHEAD):
+                for h in range(2):
+                    mx(t, g, h)
+
+        st = {}
+
+        def preadd(eng, t):
+            eng.tensor_tensor(out=resid[t][:], in0=at[t][:], in1=bf_sb[:], op=ALU.add)
+
+        def begin(t):
+            u = work.tile([P, H], F32, name="u%d" % t, tag="u")
+            sums = stats.tile([P, 4], F32, name="sums%d" % t, tag="sums%d" % t)
+            sjunk = stats.tile([P, 4], F32, name="sjunk%d" % t, tag="sjunk%d" % t)
+            nmean = stats.tile([P, 1], F32, name="nmean%d" % t, tag="nmean%d" % t)
+            ssq = stats.tile([P, 1], F32, name="ssq%d" % t, tag="ssq%d" % t)
+            std = stats.tile([P, 1], F32, name="std%d" % t, tag="std%d" % t)
+            rstd = stats.tile([P, 1], F32, name="rstd%d" % t, tag="rstd%d" % t)
+            junk = work.tile([P, H], BF16, name="junk%d" % t, tag="junk")
+            cen = work.tile([P, H], F32, name="cen%d" % t, tag="cen")
+            st[t] = (u, sums, nmean, ssq, std, rstd, junk, cen, sjunk)
+
+        def add_piece(t, k, c0, c1):
+            u, sums = st[t][0], st[t][1]
+            nc.vector.scalar_tensor_tensor(
+                out=u[:, c0:c1],
+                in0=acc[(t, k)][:, 0 : c1 - c0],
+                scalar=1.0,
+                in1=resid[t][:, c0:c1],
+                op0=ALU.mult,
+                op1=ALU.add,
+                accum_out=sums[:, k : k + 1],
+            )
+
+        def stats_on_scalar(t, npieces):
+            u, sums, nmean, ssq, std, rstd, junk, cen, sjunk = st[t]
+            nc.scalar.activation(
+                out=sjunk[:, 0:npieces], in_=sums[:, 0:npieces], func=ACT.Copy, scale=-1.0 / H, accum_out=nmean[:]
+            )
+            nc.scalar.activation(out=junk[:], in_=u[:], func=ACT.Square, bias=nmean[:, 0:1], scale=1.0, accum_out=ssq[:])
+            nc.scalar.activation(out=std[:], in_=ssq[:], func=ACT.Sqrt, bias=eps_t[:, 0:1], scale=1.0 / H)
+
+        def center(t):
+            u, nmean, cen = st[t][0], st[t][2], st[t][7]
+            nc.vector.scalar_tensor_tensor(
+                out=cen[:], in0=u[:], scalar=nmean[:, 0:1], in1=g_ps[:], op0=ALU.add, op1=ALU.mult
+            )
+
+        def recip(t):
+            nc.vector.reciprocal(out=st[t][5][:], in_=st[t][4][:])
+
+        def scale_on_scalar(t, vc):
+            rstd, cen = st[t][5], st[t][7]
+            y = work.tile([P, H - vc], F32, name="y%d" % t, tag="y")
+            nc.scalar.activation(out=y[:], in_=cen[:, vc:H], func=ACT.Copy, scale=rstd[:, 0:1])
+            return y
+
+        def affine_v(t, c0, c1):
+            rstd, cen = st[t][5], st[t][7]
+            o_v = work.tile([P, c1 - c0], F32, name="ov%d_%d" % (t, c0), tag="ov")
+            nc.vector.scalar_tensor_tensor(
+                out=o_v[:], in0=cen[:, c0:c1], scalar=rstd[:, 0:1], in1=b_ps[:, c0:c1], op0=ALU.mult, op1=ALU.add
+            )
+            nc.sync.dma_start(out=outf[P * t : P * (t + 1), c0:c1], in_=o_v[:])
+
+        def affine_g(t, vc, y):
+            o_g = work.tile([P, H - vc], F32, name="og%d" % t, tag="og")
+            nc.gpsimd.tensor_tensor(out=o_g[:], in0=y[:], in1=b_sb[:, vc:H], op=ALU.add)
+            nc.sync.dma_start(out=outf[P * t : P * (t + 1), vc:H], in_=o_g[:])
+
+        LAST = NT - 1
+        preadd(nc.vector, 0)
+        for t in range(1, 4):
+            preadd(nc.gpsimd, t)
+        for t in range(LAST):
+            begin(t)
+            add_piece(t, 0, 0, HALF)
+            if t >= 1:
+                recip(t - 1)
+                y_prev = scale_on_scalar(t - 1, VC)
+            add_piece(t, 1, HALF, H)
+            stats_on_scalar(t, 2)
+            if t >= 1:
+                affine_v(t - 1, 0, VC)
+                affine_g(t - 1, VC, y_prev)
+                if t + 3 < NT:
+                    preadd(nc.gpsimd, t + 3)
+            center(t)
+            nxt = t + NHEAD
+            if nxt < LAST:
+                open_banks(nxt)
+                for h in range(2):
+                    for g in range(NPASS):
+                        mx(nxt, g, h)
+            if nxt == LAST:
+                open_bank(LAST, 0, 2)
+                for g in range(NPASS):
+                    mx(LAST, g, 0)
+                open_bank(LAST, 1, 3)
+                for g in range(NPASS):
+                    mx(LAST, g, 1, HALF, HALF + 256)
+            if nxt == LAST + 1:
+                open_bank(LAST, 2, 4)
+                for g in range(NPASS):
+                    mx(LAST, g, 2, HALF + 256, H)
+        begin(LAST)
+        add_piece(LAST, 0, 0, HALF)
+        recip(LAST - 1)
+        y_prev = scale_on_scalar(LAST - 1, VC)
+        add_piece(LAST, 1, HALF, HALF + 256)
+        affine_v(LAST - 1, 0, VC)
+        affine_g(LAST - 1, VC, y_prev)
+        add_piece(LAST, 2, HALF + 256, H)
+        stats_on_scalar(LAST, 3)
+        center(LAST)
+        recip(LAST)
+        y_prev = scale_on_scalar(LAST, VC_LAST)
+        affine_v(LAST, 0, VC_LAST // 2)
+        affine_g(LAST, VC_LAST, y_prev)
+        affine_v(LAST, VC_LAST // 2, VC_LAST)

@@ -115,15 +115,15 @@ def tile_disentangledattention_pc_kernel(
         def load_scale_run(i):
             g0 = RUNS[i][0]
             g1 = RUNS[i][-1] + 1
-            for q in range(4):
+            for r in range(4):
                 nc.sync.dma_start(
-                    out=wpl[i][32 * q : 32 * q + 4, :, :].bitcast(I32),
-                    in_=Wf_scales[g0:g1, 4 * q : 4 * q + 4, :].rearrange("g r n -> r g n").bitcast(I32),
+                    out=wpl[i][r:P:32, :, :].bitcast(I32),
+                    in_=Wf_scales[g0:g1, r:16:4, :].rearrange("g q n -> q g n").bitcast(I32),
                 )
-            for q in range(4):
+            for r in range(4):
                 nc.sync.dma_start(
-                    out=fpl[i][32 * q : 32 * q + 4, :, :].bitcast(I32),
-                    in_=ff_scales[g0:g1, 4 * q : 4 * q + 4, 0:TH].rearrange("g r n -> r g n").bitcast(I32),
+                    out=fpl[i][r:P:32, :, :].bitcast(I32),
+                    in_=ff_scales[g0:g1, r:16:4, 0:TH].rearrange("g q n -> q g n").bitcast(I32),
                 )
 
         def load_w(g):
@@ -146,10 +146,10 @@ def tile_disentangledattention_pc_kernel(
             )
 
         def load_fplb():
-            for q in range(4):
+            for r in range(4):
                 nc.sync.dma_start(
-                    out=fplb[32 * q : 32 * q + 4, :, :].bitcast(I32),
-                    in_=ff_scales[:, 4 * q : 4 * q + 4, TH:H].rearrange("g r n -> r g n").bitcast(I32),
+                    out=fplb[r:P:32, :, :].bitcast(I32),
+                    in_=ff_scales[:, r:16:4, TH:H].rearrange("g q n -> q g n").bitcast(I32),
                 )
 
         def load_at(t):

@@ -18,13 +18,13 @@ HALF = 512
 NPASS = 8
 NT = 8
 EPS = 1e-7
-TH = 512
+TH = 384
 NHEAD = 3
-RUNS = ((0,), (1, 2, 3), (4, 5, 6, 7))
-FA_GROUPS = ((0,), (1, 2, 3), (4, 5, 6, 7))
-FB_GROUPS = ((4, 5), (6, 7))
-VC = 512
-VC_LAST = 768
+RUNS = ((0, 1), (2, 3, 4), (5, 6, 7))
+FA_GROUPS = ((0, 1), (2, 3, 4), (5, 6, 7))
+FB_GROUPS = ((3, 4), (5, 6, 7))
+VC = 640
+VC_LAST = 896
 
 
 def tile_disentangledattention_pc_kernel(
@@ -159,17 +159,17 @@ def tile_disentangledattention_pc_kernel(
         load_fa(0)
         load_scale_run(0)
         load_w(1)
+        load_w(2)
         load_fa(1)
         load_scale_run(1)
-        load_w(2)
         load_w(3)
         load_w(4)
+        load_at(0)
+        load_w(5)
         load_fa(2)
         load_scale_run(2)
-        load_w(5)
         load_w(6)
         load_w(7)
-        load_at(0)
         load_at(1)
         load_fplb()
         load_fb(0)
@@ -234,10 +234,11 @@ def tile_disentangledattention_pc_kernel(
         nc.scalar.copy(out=b_sb[:], in_=b_ps[:])
         for t in range(NHEAD):
             open_banks(t)
-        for g in range(NPASS):
+        for run in RUNS:
             for t in range(NHEAD):
-                for h in range(2):
-                    mx(t, g, h)
+                for g in run:
+                    for h in range(2):
+                        mx(t, g, h)
 
         st = {}
 

@@ -25,6 +25,7 @@ FA_GROUPS = ((0, 1), (2, 3, 4), (5, 6, 7))
 FB_GROUPS = ((3, 4), (5, 6, 7))
 VC = 640
 VC_LAST = 896
+NWARM = 5
 
 
 def tile_disentangledattention_pc_kernel(
@@ -86,6 +87,7 @@ def tile_disentangledattention_pc_kernel(
         b_sb = const.tile([P, H], BF16, name="b_sb", tag="b_sb")
         eps_t = const.tile([P, 1], F32, name="eps_t", tag="eps_t")
         warm = const.tile([P, 1], F32, name="warm", tag="warm")
+        wrm = const.tile([P, HALF], BF16, name="wrm", tag="wrm")
         g_ps = psum.tile([P, H], BF16, name="g_ps", tag="g_ps")
         b_ps = psum.tile([P, H], BF16, name="b_ps", tag="b_ps")
 
@@ -98,14 +100,15 @@ def tile_disentangledattention_pc_kernel(
             r_t = res.tile([P, H], F32, name="resid%d" % t, tag="resid%d" % t)
             resid.append(r_t)
 
-        nc.vector.memset(wpl[0][:].bitcast(I32), 0)
-        nc.vector.memset(fpl[0][:].bitcast(I32), 0)
+        nc.gpsimd.memset(fpl[0][:].bitcast(F32), 0.0)
+        nc.gpsimd.memset(wpl[0][:].bitcast(F32), 0.0)
+        nc.gpsimd.memset(wrm[:].bitcast(F32), 0.0)
+        for nm, vec in (("bf", b_f), ("g", ln2_g), ("b", ln2_b)):
+            nc.vector.memset(zrow[nm][:].bitcast(I32), 0)
+            nc.scalar.dma_start(out=zrow[nm][0:1, :], in_=vec.unsqueeze(0))
         nc.vector.memset(ones[:], 1.0)
         nc.vector.memset(eps_t[:], EPS)
-        for nm, vec in (("bf", b_f), ("g", ln2_g), ("b", ln2_b)):
-            nc.gpsimd.memset(zrow[nm][:].bitcast(F32), 0.0)
-            nc.scalar.dma_start(out=zrow[nm][0:1, :], in_=vec.unsqueeze(0))
-        nc.scalar.activation(out=warm[:], in_=eps_t[:], func=ACT.Sqrt)
+        nc.scalar.activation(out=warm[:], in_=eps_t[:], func=ACT.Abs_reciprocal_sqrt)
         for i in range(1, len(RUNS)):
             nc.vector.memset(wpl[i][:].bitcast(I32), 0)
             nc.vector.memset(fpl[i][:].bitcast(I32), 0)
@@ -117,13 +120,13 @@ def tile_disentangledattention_pc_kernel(
             g1 = RUNS[i][-1] + 1
             for r in range(4):
                 nc.sync.dma_start(
-                    out=wpl[i][r:P:32, :, :].bitcast(I32),
-                    in_=Wf_scales[g0:g1, r:16:4, :].rearrange("g q n -> q g n").bitcast(I32),
+                    out=fpl[i][r:P:32, :, :].bitcast(I32),
+                    in_=ff_scales[g0:g1, r:16:4, 0:TH].rearrange("g q n -> q g n").bitcast(I32),
                 )
             for r in range(4):
                 nc.sync.dma_start(
-                    out=fpl[i][r:P:32, :, :].bitcast(I32),
-                    in_=ff_scales[g0:g1, r:16:4, 0:TH].rearrange("g q n -> q g n").bitcast(I32),
+                    out=wpl[i][r:P:32, :, :].bitcast(I32),
+                    in_=Wf_scales[g0:g1, r:16:4, :].rearrange("g q n -> q g n").bitcast(I32),
                 )
 
         def load_w(g):
@@ -226,6 +229,9 @@ def tile_disentangledattention_pc_kernel(
                 stop=(g == NPASS - 1),
             )
 
+        dummy_ps = psum.tile([P, HALF], F32, name="dummy_ps", tag="bank0")
+        for i in range(NWARM):
+            nc.tensor.matmul(out=dummy_ps[:], lhsT=wrm[:, 0:P], rhs=wrm[:], start=True, stop=True)
         bf_ps = psum.tile([P, H], BF16, name="bf_ps", tag="bank5")
         broadcast("bf", bf_ps)
         nc.scalar.copy(out=bf_sb[:], in_=bf_ps[:])
@@ -275,7 +281,9 @@ def tile_disentangledattention_pc_kernel(
                 out=sjunk[:, 0:npieces], in_=sums[:, 0:npieces], func=ACT.Copy, scale=-1.0 / H, accum_out=nmean[:]
             )
             nc.scalar.activation(out=junk[:], in_=u[:], func=ACT.Square, bias=nmean[:, 0:1], scale=1.0, accum_out=ssq[:])
-            nc.scalar.activation(out=std[:], in_=ssq[:], func=ACT.Sqrt, bias=eps_t[:, 0:1], scale=1.0 / H)
+            nc.scalar.activation(
+                out=rstd[:], in_=ssq[:], func=ACT.Abs_reciprocal_sqrt, bias=eps_t[:, 0:1], scale=1.0 / H
+            )
 
         def center(t):
             u, nmean, cen = st[t][0], st[t][2], st[t][7]
@@ -284,7 +292,7 @@ def tile_disentangledattention_pc_kernel(
             )
 
         def recip(t):
-            nc.vector.reciprocal(out=st[t][5][:], in_=st[t][4][:])
+            return None
 
         def scale_on_scalar(t, vc):
             rstd, cen = st[t][5], st[t][7]

@@ -18,11 +18,14 @@ HALF = 512
 NPASS = 8
 NT = 8
 EPS = 1e-7
-TH = 384
+TH = 512
 NHEAD = 3
+NSPLIT = 4
+GA = (0, 1, 2, 3, 4)
+GB = (5, 6, 7)
 RUNS = ((0, 1), (2, 3, 4), (5, 6, 7))
 FA_GROUPS = ((0, 1), (2, 3, 4), (5, 6, 7))
-FB_GROUPS = ((3, 4), (5, 6, 7))
+FB_GROUPS = ((4, 5), (6, 7))
 VC = 640
 VC_LAST = 896
 NWARM = 5
@@ -167,17 +170,17 @@ def tile_disentangledattention_pc_kernel(
         load_scale_run(1)
         load_w(3)
         load_w(4)
-        load_at(0)
         load_w(5)
         load_fa(2)
         load_scale_run(2)
+        load_at(0)
         load_w(6)
         load_w(7)
         load_at(1)
-        load_fplb()
-        load_fb(0)
         load_at(2)
         load_at(3)
+        load_fplb()
+        load_fb(0)
         load_fb(1)
         load_at(4)
         load_at(5)
@@ -198,14 +201,14 @@ def tile_disentangledattention_pc_kernel(
         acc = {}
 
         def open_bank(t, k, bank):
-            a_tk = psum.tile([P, HALF], F32, name="acc%d_%d" % (t, k), tag="bank%d" % bank)
+            a_tk = psum.tile([P, HALF], F32, name="acc%d_%d_b%d" % (t, k, bank), tag="bank%d" % bank)
             acc[(t, k)] = a_tk
 
-        def open_banks(t):
+        def open_pair(t, pair):
             for h in range(2):
-                open_bank(t, h, 2 * (t % 3) + h)
+                open_bank(t, h, 2 * pair + h)
 
-        def mx(t, g, k, c0=None, c1=None):
+        def mx(t, g, k, c0=None, c1=None, first=0, last=NPASS - 1):
             if c0 is None:
                 c0 = HALF * k
                 c1 = HALF * (k + 1)
@@ -225,8 +228,8 @@ def tile_disentangledattention_pc_kernel(
                 lhsT_scale=lhs_s,
                 rhs=wc[g][:, 2 * c0 : 2 * c1].bitcast(FP4),
                 rhs_scale=wpl[i][:, j, c0:c1],
-                start=(g == 0),
-                stop=(g == NPASS - 1),
+                start=(g == first),
+                stop=(g == last),
             )
 
         dummy_ps = psum.tile([P, HALF], F32, name="dummy_ps", tag="bank0")
@@ -239,17 +242,39 @@ def tile_disentangledattention_pc_kernel(
         broadcast("b", b_ps)
         nc.scalar.copy(out=b_sb[:], in_=b_ps[:])
         for t in range(NHEAD):
-            open_banks(t)
-        for run in RUNS:
+            open_pair(t, t)
+        for run in RUNS[:-1]:
             for t in range(NHEAD):
                 for g in run:
                     for h in range(2):
-                        mx(t, g, h)
+                        mx(t, g, h, None, None, GA[0], GA[-1])
 
         st = {}
 
+        part = {}
+
         def preadd(eng, t):
-            eng.tensor_tensor(out=resid[t][:], in0=at[t][:], in1=bf_sb[:], op=ALU.add)
+            if t < NSPLIT:
+                eng.tensor_tensor(out=resid[t][:], in0=at[t][:], in1=part[t][:], op=ALU.add)
+            else:
+                eng.tensor_tensor(out=resid[t][:], in0=at[t][:], in1=bf_sb[:], op=ALU.add)
+
+        def empty_first_part(t):
+            p_t = res.tile([P, H], F32, name="part%d" % t, tag="part%d" % t)
+            part[t] = p_t
+            for h in range(2):
+                nc.vector.tensor_tensor(
+                    out=p_t[:, HALF * h : HALF * (h + 1)],
+                    in0=acc[(t, h)][:],
+                    in1=bf_sb[:, HALF * h : HALF * (h + 1)],
+                    op=ALU.add,
+                )
+
+        def second_part(t, pair):
+            open_pair(t, pair)
+            for g in GB:
+                for h in range(2):
+                    mx(t, g, h, None, None, GB[0], GB[-1])
 
         def begin(t):
             u = work.tile([P, H], F32, name="u%d" % t, tag="u")
@@ -314,9 +339,21 @@ def tile_disentangledattention_pc_kernel(
             nc.sync.dma_start(out=outf[P * t : P * (t + 1), vc:H], in_=o_g[:])
 
         LAST = NT - 1
+        empty_first_part(0)
+        open_pair(3, 0)
+        for h in range(2):
+            for g in GA:
+                mx(3, g, h, None, None, GA[0], GA[-1])
+        empty_first_part(1)
+        second_part(0, 1)
+        empty_first_part(2)
+        second_part(1, 2)
         preadd(nc.vector, 0)
-        for t in range(1, 4):
-            preadd(nc.gpsimd, t)
+        preadd(nc.gpsimd, 1)
+        preadd(nc.gpsimd, 2)
+        empty_first_part(3)
+        second_part(2, 0)
+        preadd(nc.gpsimd, 3)
         for t in range(LAST):
             begin(t)
             add_piece(t, 0, 0, HALF)
@@ -331,21 +368,23 @@ def tile_disentangledattention_pc_kernel(
                 if t + 3 < NT:
                     preadd(nc.gpsimd, t + 3)
             center(t)
-            nxt = t + NHEAD
-            if nxt < LAST:
-                open_banks(nxt)
+            nxt = t + 3
+            if nxt == 3:
+                second_part(3, 1)
+            elif nxt < LAST:
+                open_pair(nxt, (nxt + 1) % 3)
                 for h in range(2):
                     for g in range(NPASS):
                         mx(nxt, g, h)
             if nxt == LAST:
-                open_bank(LAST, 0, 2)
+                open_bank(LAST, 0, 4)
                 for g in range(NPASS):
                     mx(LAST, g, 0)
-                open_bank(LAST, 1, 3)
+                open_bank(LAST, 1, 5)
                 for g in range(NPASS):
                     mx(LAST, g, 1, HALF, HALF + 256)
             if nxt == LAST + 1:
-                open_bank(LAST, 2, 4)
+                open_bank(LAST, 2, 0)
                 for g in range(NPASS):
                     mx(LAST, g, 2, HALF + 256, H)
         begin(LAST)

@@ -21,14 +21,12 @@ EPS = 1e-7
 TH = 512
 NHEAD = 3
 NSPLIT = 4
-GA = (0, 1, 2, 3, 4)
-GB = (5, 6, 7)
 RUNS = ((0, 1), (2, 3, 4), (5, 6, 7))
 FA_GROUPS = ((0, 1), (2, 3, 4), (5, 6, 7))
 FB_GROUPS = ((4, 5), (6, 7))
 VC = 640
 VC_LAST = 896
-NWARM = 5
+NWARM = 4
 
 
 def tile_disentangledattention_pc_kernel(
@@ -103,9 +101,9 @@ def tile_disentangledattention_pc_kernel(
             r_t = res.tile([P, H], F32, name="resid%d" % t, tag="resid%d" % t)
             resid.append(r_t)
 
+        nc.gpsimd.memset(wrm[:].bitcast(F32), 0.0)
         nc.gpsimd.memset(fpl[0][:].bitcast(F32), 0.0)
         nc.gpsimd.memset(wpl[0][:].bitcast(F32), 0.0)
-        nc.gpsimd.memset(wrm[:].bitcast(F32), 0.0)
         for nm, vec in (("bf", b_f), ("g", ln2_g), ("b", ln2_b)):
             nc.vector.memset(zrow[nm][:].bitcast(I32), 0)
             nc.scalar.dma_start(out=zrow[nm][0:1, :], in_=vec.unsqueeze(0))
@@ -170,13 +168,13 @@ def tile_disentangledattention_pc_kernel(
         load_scale_run(1)
         load_w(3)
         load_w(4)
+        load_at(0)
         load_w(5)
         load_fa(2)
         load_scale_run(2)
-        load_at(0)
+        load_at(1)
         load_w(6)
         load_w(7)
-        load_at(1)
         load_at(2)
         load_at(3)
         load_fplb()
@@ -241,13 +239,20 @@ def tile_disentangledattention_pc_kernel(
         broadcast("g", g_ps)
         broadcast("b", b_ps)
         nc.scalar.copy(out=b_sb[:], in_=b_ps[:])
-        for t in range(NHEAD):
-            open_pair(t, t)
-        for run in RUNS[:-1]:
-            for t in range(NHEAD):
-                for g in run:
-                    for h in range(2):
-                        mx(t, g, h, None, None, GA[0], GA[-1])
+        units = []
+        for r in range(len(RUNS)):
+            for t in range(NSPLIT):
+                units.append((t, r))
+
+        def run_unit(j):
+            t, r = units[j]
+            open_pair(t, j % 3)
+            for g in RUNS[r]:
+                for h in range(2):
+                    mx(t, g, h, None, None, RUNS[r][0], RUNS[r][-1])
+
+        for j in range(3):
+            run_unit(j)
 
         st = {}
 
@@ -259,22 +264,17 @@ def tile_disentangledattention_pc_kernel(
             else:
                 eng.tensor_tensor(out=resid[t][:], in0=at[t][:], in1=bf_sb[:], op=ALU.add)
 
-        def empty_first_part(t):
-            p_t = res.tile([P, H], F32, name="part%d" % t, tag="part%d" % t)
-            part[t] = p_t
+        def empty_part(t, r):
+            p_t = res.tile([P, H], F32, name="part%d_%d" % (t, r), tag="part%d_%d" % (t, r))
+            before = bf_sb if r == 0 else part[t]
             for h in range(2):
                 nc.vector.tensor_tensor(
                     out=p_t[:, HALF * h : HALF * (h + 1)],
                     in0=acc[(t, h)][:],
-                    in1=bf_sb[:, HALF * h : HALF * (h + 1)],
+                    in1=before[:, HALF * h : HALF * (h + 1)],
                     op=ALU.add,
                 )
-
-        def second_part(t, pair):
-            open_pair(t, pair)
-            for g in GB:
-                for h in range(2):
-                    mx(t, g, h, None, None, GB[0], GB[-1])
+            part[t] = p_t
 
         def begin(t):
             u = work.tile([P, H], F32, name="u%d" % t, tag="u")
@@ -339,21 +339,12 @@ def tile_disentangledattention_pc_kernel(
             nc.sync.dma_start(out=outf[P * t : P * (t + 1), vc:H], in_=o_g[:])
 
         LAST = NT - 1
-        empty_first_part(0)
-        open_pair(3, 0)
-        for h in range(2):
-            for g in GA:
-                mx(3, g, h, None, None, GA[0], GA[-1])
-        empty_first_part(1)
-        second_part(0, 1)
-        empty_first_part(2)
-        second_part(1, 2)
-        preadd(nc.vector, 0)
-        preadd(nc.gpsimd, 1)
-        preadd(nc.gpsimd, 2)
-        empty_first_part(3)
-        second_part(2, 0)
-        preadd(nc.gpsimd, 3)
+        for j in range(2 * NSPLIT):
+            t, r = units[j]
+            empty_part(t, r)
+            if r == 1:
+                preadd(nc.gpsimd, t)
+            run_unit(j + 3)
         for t in range(LAST):
             begin(t)
             add_piece(t, 0, 0, HALF)
@@ -370,21 +361,21 @@ def tile_disentangledattention_pc_kernel(
             center(t)
             nxt = t + 3
             if nxt == 3:
-                second_part(3, 1)
+                run_unit(3 * NSPLIT - 1)
             elif nxt < LAST:
-                open_pair(nxt, (nxt + 1) % 3)
+                open_pair(nxt, (nxt + 2) % 3)
                 for h in range(2):
                     for g in range(NPASS):
                         mx(nxt, g, h)
             if nxt == LAST:
-                open_bank(LAST, 0, 4)
+                open_bank(LAST, 0, 0)
                 for g in range(NPASS):
                     mx(LAST, g, 0)
-                open_bank(LAST, 1, 5)
+                open_bank(LAST, 1, 1)
                 for g in range(NPASS):
                     mx(LAST, g, 1, HALF, HALF + 256)
             if nxt == LAST + 1:
-                open_bank(LAST, 2, 0)
+                open_bank(LAST, 2, 2)
                 for g in range(NPASS):
                     mx(LAST, g, 2, HALF + 256, H)
         begin(LAST)

@@ -13,20 +13,28 @@ ALU = mybir.AluOpType
 ACT = mybir.ActivationFunctionType
 
 P = 128
+QUADRANT = 32
+ROWS_PER_QUADRANT = 4
+SCALE_ROWS = 16
 H = 1024
-HALF = 512
-NPASS = 8
-NT = 8
+BANK = 512
+N_PASS = 8
+N_TILES = 8
+LAST = N_TILES - 1
 EPS = 1e-7
-TH = 512
-NHEAD = 3
-NSPLIT = 4
+
 RUNS = ((0, 1), (2, 3, 4), (5, 6, 7))
-FA_GROUPS = ((0, 1), (2, 3, 4), (5, 6, 7))
-FB_GROUPS = ((4, 5), (6, 7))
-VC = 640
-VC_LAST = 896
-NWARM = 4
+N_RIDERS = 4
+RIDER_TOKENS = P * N_RIDERS
+LATE_TILES = ((4, 5), (6, 7))
+N_PAIRS = 3
+
+ADDEND_AHEAD = 3
+
+V_COLS = 544
+V_COLS_LAST = 896
+LAST_PIECES = ((0, 512), (512, 768), (768, 1024))
+N_WARM = 4
 
 
 def tile_disentangledattention_pc_kernel(
@@ -34,362 +42,361 @@ def tile_disentangledattention_pc_kernel(
 ):
     nc = tc.nc
     attn = attn_out.flatten_outer_dims()
-    outf = out.flatten_outer_dims()
+    out_rows = out.flatten_outer_dims()
 
     with ExitStack() as ctx:
         const = ctx.enter_context(tc.tile_pool(name="const", bufs=1))
         codes = ctx.enter_context(tc.tile_pool(name="codes", bufs=1))
         planes = ctx.enter_context(tc.tile_pool(name="planes", bufs=1))
-        res = ctx.enter_context(tc.tile_pool(name="res", bufs=1))
+        keep = ctx.enter_context(tc.tile_pool(name="keep", bufs=1))
         work = ctx.enter_context(tc.tile_pool(name="work", bufs=3))
         stats = ctx.enter_context(tc.tile_pool(name="stats", bufs=1))
         psum = ctx.enter_context(tc.psum_pool(name="psum", bufs=1))
         ctx.enter_context(tc.manual_schedule())
 
-        wpl = []
-        fpl = []
+        def own_tile(pool, shape, dtype, name):
+            return pool.tile(shape, dtype, name=name, tag=name)
+
+        def operand_tile(pool, shape, name):
+            return pool.tile(shape, U8, name=name, tag=name, align_bytes=64)
+
+        w_plane = []
+        rider_plane = []
         for i, run in enumerate(RUNS):
-            wpl_i = planes.tile([P, len(run), H], U8, name="wpl%d" % i, tag="wpl%d" % i, align_bytes=64)
-            fpl_i = planes.tile([P, len(run), TH], U8, name="fpl%d" % i, tag="fpl%d" % i, align_bytes=64)
-            wpl.append(wpl_i)
-            fpl.append(fpl_i)
-        fplb = planes.tile([P, NPASS, H - TH], U8, name="fplb", tag="fplb", align_bytes=64)
-        wc = []
-        for g in range(NPASS):
-            wc_g = codes.tile([P, 2 * H], U8, name="wc%d" % g, tag="wc%d" % g, align_bytes=64)
-            wc.append(wc_g)
-        fa = []
-        for i, grp in enumerate(FA_GROUPS):
-            fa_i = codes.tile([P, len(grp), 2 * TH], U8, name="fa%d" % i, tag="fa%d" % i, align_bytes=64)
-            fa.append(fa_i)
-        fb = []
-        for i, grp in enumerate(FB_GROUPS):
-            fb_i = codes.tile([P, NPASS, 256 * len(grp)], U8, name="fb%d" % i, tag="fb%d" % i, align_bytes=64)
-            fb.append(fb_i)
-        run_of = {}
+            w_plane.append(operand_tile(planes, [P, len(run), H], "w_plane%d" % i))
+            rider_plane.append(operand_tile(planes, [P, len(run), RIDER_TOKENS], "rider_plane%d" % i))
+        late_plane = operand_tile(planes, [P, N_PASS, H - RIDER_TOKENS], "late_plane")
+        w_codes = []
+        for g in range(N_PASS):
+            w_codes.append(operand_tile(codes, [P, 2 * H], "w_codes%d" % g))
+        rider_codes = []
+        for i, run in enumerate(RUNS):
+            rider_codes.append(operand_tile(codes, [P, len(run), 2 * RIDER_TOKENS], "rider_codes%d" % i))
+        late_codes = []
+        for a, tiles in enumerate(LATE_TILES):
+            late_codes.append(operand_tile(codes, [P, N_PASS, 2 * P * len(tiles)], "late_codes%d" % a))
+        place_in_run = {}
         for i, run in enumerate(RUNS):
             for j, g in enumerate(run):
-                run_of[g] = (i, j)
-        fa_of = {}
-        for i, grp in enumerate(FA_GROUPS):
-            for j, g in enumerate(grp):
-                fa_of[g] = (i, j)
-        fb_of = {}
-        for i, grp in enumerate(FB_GROUPS):
-            for j, t in enumerate(grp):
-                fb_of[t] = (i, j)
+                place_in_run[g] = (i, j)
+        place_in_load = {}
+        for a, tiles in enumerate(LATE_TILES):
+            for b, t in enumerate(tiles):
+                place_in_load[t] = (a, b)
 
-        ones = const.tile([P, P], BF16, name="ones", tag="ones")
-        zrow = {}
-        for nm in ("bf", "g", "b"):
-            z_nm = const.tile([P, H], BF16, name="z_%s" % nm, tag="z_%s" % nm)
-            zrow[nm] = z_nm
-        bf_sb = const.tile([P, H], BF16, name="bf_sb", tag="bf_sb")
-        b_sb = const.tile([P, H], BF16, name="b_sb", tag="b_sb")
-        eps_t = const.tile([P, 1], F32, name="eps_t", tag="eps_t")
-        warm = const.tile([P, 1], F32, name="warm", tag="warm")
-        wrm = const.tile([P, HALF], BF16, name="wrm", tag="wrm")
-        g_ps = psum.tile([P, H], BF16, name="g_ps", tag="g_ps")
-        b_ps = psum.tile([P, H], BF16, name="b_ps", tag="b_ps")
+        ones = own_tile(const, [P, P], BF16, "ones")
+        vec_row = {}
+        for nm in ("b_f", "ln2_g", "ln2_b"):
+            vec_row[nm] = own_tile(const, [P, H], BF16, "row_%s" % nm)
+        b_f_all = own_tile(const, [P, H], BF16, "b_f_all")
+        ln2_b_all = own_tile(const, [P, H], BF16, "ln2_b_all")
+        eps_col = own_tile(const, [P, 1], F32, "eps_col")
+        table_warm = own_tile(const, [P, 1], F32, "table_warm")
+        zeros = own_tile(const, [P, BANK], BF16, "zeros")
+        g_bank = own_tile(psum, [P, H], BF16, "g_bank")
+        b_bank = own_tile(psum, [P, H], BF16, "b_bank")
 
-        at = []
-        for t in range(NT):
-            at_t = res.tile([P, H], BF16, name="at%d" % t, tag="at%d" % t)
-            at.append(at_t)
-        resid = []
-        for t in range(NT):
-            r_t = res.tile([P, H], F32, name="resid%d" % t, tag="resid%d" % t)
-            resid.append(r_t)
+        attn_sb = []
+        for t in range(N_TILES):
+            attn_sb.append(own_tile(keep, [P, H], BF16, "attn%d" % t))
+        addend = []
+        for t in range(N_TILES):
+            addend.append(own_tile(keep, [P, H], F32, "addend%d" % t))
 
-        nc.gpsimd.memset(wrm[:].bitcast(F32), 0.0)
-        nc.gpsimd.memset(fpl[0][:].bitcast(F32), 0.0)
-        nc.gpsimd.memset(wpl[0][:].bitcast(F32), 0.0)
-        for nm, vec in (("bf", b_f), ("g", ln2_g), ("b", ln2_b)):
-            nc.vector.memset(zrow[nm][:].bitcast(I32), 0)
-            nc.scalar.dma_start(out=zrow[nm][0:1, :], in_=vec.unsqueeze(0))
+        nc.gpsimd.memset(zeros[:].bitcast(F32), 0.0)
+        nc.gpsimd.memset(rider_plane[0][:].bitcast(F32), 0.0)
+        nc.gpsimd.memset(w_plane[0][:].bitcast(F32), 0.0)
+        for nm, vec in (("b_f", b_f), ("ln2_g", ln2_g), ("ln2_b", ln2_b)):
+            nc.vector.memset(vec_row[nm][:].bitcast(I32), 0)
+            nc.scalar.dma_start(out=vec_row[nm][0:1, :], in_=vec.unsqueeze(0))
         nc.vector.memset(ones[:], 1.0)
-        nc.vector.memset(eps_t[:], EPS)
-        nc.scalar.activation(out=warm[:], in_=eps_t[:], func=ACT.Abs_reciprocal_sqrt)
+        nc.vector.memset(eps_col[:], EPS)
+        nc.scalar.activation(out=table_warm[:], in_=eps_col[:], func=ACT.Abs_reciprocal_sqrt)
         for i in range(1, len(RUNS)):
-            nc.vector.memset(wpl[i][:].bitcast(I32), 0)
-            nc.vector.memset(fpl[i][:].bitcast(I32), 0)
-        nc.vector.memset(fplb[:].bitcast(I32), 0)
+            nc.vector.memset(w_plane[i][:].bitcast(I32), 0)
+            nc.vector.memset(rider_plane[i][:].bitcast(I32), 0)
+        nc.vector.memset(late_plane[:].bitcast(I32), 0)
 
+        def load_scale_rows(plane, scales, g0, g1, n0, n1):
+            for r in range(ROWS_PER_QUADRANT):
+                nc.sync.dma_start(
+                    out=plane[r:P:QUADRANT, :, :].bitcast(I32),
+                    in_=scales[g0:g1, r:SCALE_ROWS:ROWS_PER_QUADRANT, n0:n1].rearrange("g q n -> q g n").bitcast(I32),
+                )
 
-        def load_scale_run(i):
+        def load_run_scales(i):
             g0 = RUNS[i][0]
             g1 = RUNS[i][-1] + 1
-            for r in range(4):
-                nc.sync.dma_start(
-                    out=fpl[i][r:P:32, :, :].bitcast(I32),
-                    in_=ff_scales[g0:g1, r:16:4, 0:TH].rearrange("g q n -> q g n").bitcast(I32),
-                )
-            for r in range(4):
-                nc.sync.dma_start(
-                    out=wpl[i][r:P:32, :, :].bitcast(I32),
-                    in_=Wf_scales[g0:g1, r:16:4, :].rearrange("g q n -> q g n").bitcast(I32),
-                )
+            load_scale_rows(rider_plane[i], ff_scales, g0, g1, 0, RIDER_TOKENS)
+            load_scale_rows(w_plane[i], Wf_scales, g0, g1, 0, H)
 
-        def load_w(g):
-            nc.sync.dma_start(out=wc[g][:].bitcast(I32), in_=Wf_words[g].bitcast(I32))
+        def load_w_codes(g):
+            nc.sync.dma_start(out=w_codes[g][:].bitcast(I32), in_=Wf_words[g].bitcast(I32))
 
-        def load_fa(i):
-            g0 = FA_GROUPS[i][0]
-            g1 = FA_GROUPS[i][-1] + 1
+        def load_rider_codes(i):
+            g0 = RUNS[i][0]
+            g1 = RUNS[i][-1] + 1
             nc.sync.dma_start(
-                out=fa[i][:].bitcast(I32),
-                in_=ff_words[g0:g1, :, 0 : 2 * TH].rearrange("g p n -> p g n").bitcast(I32),
+                out=rider_codes[i][:].bitcast(I32),
+                in_=ff_words[g0:g1, :, 0 : 2 * RIDER_TOKENS].rearrange("g p n -> p g n").bitcast(I32),
             )
 
-        def load_fb(i):
-            t0 = FB_GROUPS[i][0]
-            t1 = FB_GROUPS[i][-1] + 1
+        def load_late_codes(a):
+            t0 = LATE_TILES[a][0]
+            t1 = LATE_TILES[a][-1] + 1
             nc.sync.dma_start(
-                out=fb[i][:].bitcast(I32),
-                in_=ff_words[:, :, 256 * t0 : 256 * t1].rearrange("g p n -> p g n").bitcast(I32),
+                out=late_codes[a][:].bitcast(I32),
+                in_=ff_words[:, :, 2 * P * t0 : 2 * P * t1].rearrange("g p n -> p g n").bitcast(I32),
             )
 
-        def load_fplb():
-            for r in range(4):
-                nc.sync.dma_start(
-                    out=fplb[r:P:32, :, :].bitcast(I32),
-                    in_=ff_scales[:, r:16:4, TH:H].rearrange("g q n -> q g n").bitcast(I32),
-                )
+        def load_attn(t):
+            nc.sync.dma_start(out=attn_sb[t][:], in_=attn[P * t : P * (t + 1), :])
 
-        def load_at(t):
-            nc.sync.dma_start(out=at[t][:], in_=attn[P * t : P * (t + 1), :])
+        load_w_codes(0)
+        load_rider_codes(0)
+        load_run_scales(0)
+        load_w_codes(1)
+        load_w_codes(2)
+        load_rider_codes(1)
+        load_run_scales(1)
+        load_w_codes(3)
+        load_w_codes(4)
+        load_attn(0)
+        load_w_codes(5)
+        load_rider_codes(2)
+        load_run_scales(2)
+        load_attn(1)
+        load_w_codes(6)
+        load_w_codes(7)
+        load_attn(2)
+        load_attn(3)
+        load_scale_rows(late_plane, ff_scales, 0, N_PASS, RIDER_TOKENS, H)
+        load_late_codes(0)
+        load_late_codes(1)
+        for t in range(N_RIDERS, N_TILES):
+            load_attn(t)
 
-        load_w(0)
-        load_fa(0)
-        load_scale_run(0)
-        load_w(1)
-        load_w(2)
-        load_fa(1)
-        load_scale_run(1)
-        load_w(3)
-        load_w(4)
-        load_at(0)
-        load_w(5)
-        load_fa(2)
-        load_scale_run(2)
-        load_at(1)
-        load_w(6)
-        load_w(7)
-        load_at(2)
-        load_at(3)
-        load_fplb()
-        load_fb(0)
-        load_fb(1)
-        load_at(4)
-        load_at(5)
-        load_at(6)
-        load_at(7)
-
-        def broadcast(nm, dst):
+        def spread(nm, dst):
             for h in range(2):
                 nc.tensor.matmul(
-                    out=dst[:, HALF * h : HALF * (h + 1)],
+                    out=dst[:, BANK * h : BANK * (h + 1)],
                     lhsT=ones[:],
-                    rhs=zrow[nm][:, HALF * h : HALF * (h + 1)],
+                    rhs=vec_row[nm][:, BANK * h : BANK * (h + 1)],
                     start=True,
                     stop=True,
                 )
 
+        warm_bank = psum.tile([P, BANK], F32, name="warm_bank", tag="bank0")
+        for rep in range(N_WARM):
+            nc.tensor.matmul(out=warm_bank[:], lhsT=zeros[:, 0:P], rhs=zeros[:], start=True, stop=True)
+        b_f_bank = psum.tile([P, H], BF16, name="b_f_bank", tag="bank5")
+        spread("b_f", b_f_bank)
+        nc.scalar.copy(out=b_f_all[:], in_=b_f_bank[:])
+        spread("ln2_g", g_bank)
+        spread("ln2_b", b_bank)
+        nc.scalar.copy(out=ln2_b_all[:], in_=b_bank[:])
 
-        acc = {}
+        group = {}
 
-        def open_bank(t, k, bank):
-            a_tk = psum.tile([P, HALF], F32, name="acc%d_%d_b%d" % (t, k, bank), tag="bank%d" % bank)
-            acc[(t, k)] = a_tk
+        def open_group(t, piece, bank):
+            group[(t, piece)] = psum.tile(
+                [P, BANK], F32, name="group%d_%d_bank%d" % (t, piece, bank), tag="bank%d" % bank
+            )
 
         def open_pair(t, pair):
             for h in range(2):
-                open_bank(t, h, 2 * pair + h)
+                open_group(t, h, 2 * pair + h)
 
-        def mx(t, g, k, c0=None, c1=None, first=0, last=NPASS - 1):
-            if c0 is None:
-                c0 = HALF * k
-                c1 = HALF * (k + 1)
-            if P * t < TH:
-                i, j = fa_of[g]
-                lhs = fa[i][:, j, 256 * t : 256 * (t + 1)]
-                i, j = run_of[g]
-                lhs_s = fpl[i][:, j, P * t : P * (t + 1)]
+        def multiply(t, g, piece, c0, c1, first, last):
+            i, j = place_in_run[g]
+            if t < N_RIDERS:
+                tokens = rider_codes[i][:, j, 2 * P * t : 2 * P * (t + 1)]
+                token_scales = rider_plane[i][:, j, P * t : P * (t + 1)]
             else:
-                i, j = fb_of[t]
-                lhs = fb[i][:, g, 256 * j : 256 * (j + 1)]
-                lhs_s = fplb[:, g, P * t - TH : P * (t + 1) - TH]
-            i, j = run_of[g]
+                a, b = place_in_load[t]
+                tokens = late_codes[a][:, g, 2 * P * b : 2 * P * (b + 1)]
+                token_scales = late_plane[:, g, P * t - RIDER_TOKENS : P * (t + 1) - RIDER_TOKENS]
             nc.tensor.matmul_mx(
-                out=acc[(t, k)][:, 0 : c1 - c0],
-                lhsT=lhs.bitcast(FP4),
-                lhsT_scale=lhs_s,
-                rhs=wc[g][:, 2 * c0 : 2 * c1].bitcast(FP4),
-                rhs_scale=wpl[i][:, j, c0:c1],
+                out=group[(t, piece)][:, 0 : c1 - c0],
+                lhsT=tokens.bitcast(FP4),
+                lhsT_scale=token_scales,
+                rhs=w_codes[g][:, 2 * c0 : 2 * c1].bitcast(FP4),
+                rhs_scale=w_plane[i][:, j, c0:c1],
                 start=(g == first),
                 stop=(g == last),
             )
 
-        dummy_ps = psum.tile([P, HALF], F32, name="dummy_ps", tag="bank0")
-        for i in range(NWARM):
-            nc.tensor.matmul(out=dummy_ps[:], lhsT=wrm[:, 0:P], rhs=wrm[:], start=True, stop=True)
-        bf_ps = psum.tile([P, H], BF16, name="bf_ps", tag="bank5")
-        broadcast("bf", bf_ps)
-        nc.scalar.copy(out=bf_sb[:], in_=bf_ps[:])
-        broadcast("g", g_ps)
-        broadcast("b", b_ps)
-        nc.scalar.copy(out=b_sb[:], in_=b_ps[:])
-        units = []
-        for r in range(len(RUNS)):
-            for t in range(NSPLIT):
-                units.append((t, r))
+        rides = []
+        for i in range(len(RUNS)):
+            for t in range(N_RIDERS):
+                rides.append((t, i))
 
-        def run_unit(j):
-            t, r = units[j]
-            open_pair(t, j % 3)
-            for g in RUNS[r]:
+        def ride(m):
+            t, i = rides[m]
+            open_pair(t, m % N_PAIRS)
+            for g in RUNS[i]:
                 for h in range(2):
-                    mx(t, g, h, None, None, RUNS[r][0], RUNS[r][-1])
+                    multiply(t, g, h, BANK * h, BANK * (h + 1), RUNS[i][0], RUNS[i][-1])
 
-        for j in range(3):
-            run_unit(j)
+        def whole_tile(t, pair):
+            open_pair(t, pair)
+            for h in range(2):
+                for g in range(N_PASS):
+                    multiply(t, g, h, BANK * h, BANK * (h + 1), 0, N_PASS - 1)
 
-        st = {}
+        def last_tile_piece(piece, bank):
+            c0, c1 = LAST_PIECES[piece]
+            open_group(LAST, piece, bank)
+            for g in range(N_PASS):
+                multiply(LAST, g, piece, c0, c1, 0, N_PASS - 1)
 
-        part = {}
+        partial = {}
 
-        def preadd(eng, t):
-            if t < NSPLIT:
-                eng.tensor_tensor(out=resid[t][:], in0=at[t][:], in1=part[t][:], op=ALU.add)
-            else:
-                eng.tensor_tensor(out=resid[t][:], in0=at[t][:], in1=bf_sb[:], op=ALU.add)
-
-        def empty_part(t, r):
-            p_t = res.tile([P, H], F32, name="part%d_%d" % (t, r), tag="part%d_%d" % (t, r))
-            before = bf_sb if r == 0 else part[t]
+        def add_to_partial(t, i):
+            so_far = b_f_all if i == 0 else partial[t]
+            partial[t] = own_tile(keep, [P, H], F32, "partial%d_%d" % (t, i))
             for h in range(2):
                 nc.vector.tensor_tensor(
-                    out=p_t[:, HALF * h : HALF * (h + 1)],
-                    in0=acc[(t, h)][:],
-                    in1=before[:, HALF * h : HALF * (h + 1)],
+                    out=partial[t][:, BANK * h : BANK * (h + 1)],
+                    in0=group[(t, h)][:],
+                    in1=so_far[:, BANK * h : BANK * (h + 1)],
                     op=ALU.add,
                 )
-            part[t] = p_t
+
+        def make_addend(t):
+            rest = partial[t] if t < N_RIDERS else b_f_all
+            nc.gpsimd.tensor_tensor(out=addend[t][:], in0=attn_sb[t][:], in1=rest[:], op=ALU.add)
+
+        tiles_of = {}
 
         def begin(t):
-            u = work.tile([P, H], F32, name="u%d" % t, tag="u")
-            sums = stats.tile([P, 4], F32, name="sums%d" % t, tag="sums%d" % t)
-            sjunk = stats.tile([P, 4], F32, name="sjunk%d" % t, tag="sjunk%d" % t)
-            nmean = stats.tile([P, 1], F32, name="nmean%d" % t, tag="nmean%d" % t)
-            ssq = stats.tile([P, 1], F32, name="ssq%d" % t, tag="ssq%d" % t)
-            std = stats.tile([P, 1], F32, name="std%d" % t, tag="std%d" % t)
-            rstd = stats.tile([P, 1], F32, name="rstd%d" % t, tag="rstd%d" % t)
-            junk = work.tile([P, H], BF16, name="junk%d" % t, tag="junk")
-            cen = work.tile([P, H], F32, name="cen%d" % t, tag="cen")
-            st[t] = (u, sums, nmean, ssq, std, rstd, junk, cen, sjunk)
+            tiles_of[t] = {
+                "u": work.tile([P, H], F32, name="u%d" % t, tag="u"),
+                "row_sums": own_tile(stats, [P, len(LAST_PIECES)], F32, "row_sums%d" % t),
+                "scaled_sums": own_tile(stats, [P, len(LAST_PIECES)], F32, "scaled_sums%d" % t),
+                "neg_mean": own_tile(stats, [P, 1], F32, "neg_mean%d" % t),
+                "sum_sq": own_tile(stats, [P, 1], F32, "sum_sq%d" % t),
+                "rstd": own_tile(stats, [P, 1], F32, "rstd%d" % t),
+                "squares": work.tile([P, H], BF16, name="squares%d" % t, tag="squares"),
+                "centred": work.tile([P, H], F32, name="centred%d" % t, tag="centred"),
+            }
 
-        def add_piece(t, k, c0, c1):
-            u, sums = st[t][0], st[t][1]
+        def empty_group(t, piece, c0, c1):
+            own = tiles_of[t]
             nc.vector.scalar_tensor_tensor(
-                out=u[:, c0:c1],
-                in0=acc[(t, k)][:, 0 : c1 - c0],
+                out=own["u"][:, c0:c1],
+                in0=group[(t, piece)][:, 0 : c1 - c0],
                 scalar=1.0,
-                in1=resid[t][:, c0:c1],
+                in1=addend[t][:, c0:c1],
                 op0=ALU.mult,
                 op1=ALU.add,
-                accum_out=sums[:, k : k + 1],
+                accum_out=own["row_sums"][:, piece : piece + 1],
             )
 
-        def stats_on_scalar(t, npieces):
-            u, sums, nmean, ssq, std, rstd, junk, cen, sjunk = st[t]
+        def row_stats(t, n_pieces):
+            own = tiles_of[t]
             nc.scalar.activation(
-                out=sjunk[:, 0:npieces], in_=sums[:, 0:npieces], func=ACT.Copy, scale=-1.0 / H, accum_out=nmean[:]
+                out=own["scaled_sums"][:, 0:n_pieces],
+                in_=own["row_sums"][:, 0:n_pieces],
+                func=ACT.Copy,
+                scale=-1.0 / H,
+                accum_out=own["neg_mean"][:],
             )
-            nc.scalar.activation(out=junk[:], in_=u[:], func=ACT.Square, bias=nmean[:, 0:1], scale=1.0, accum_out=ssq[:])
             nc.scalar.activation(
-                out=rstd[:], in_=ssq[:], func=ACT.Abs_reciprocal_sqrt, bias=eps_t[:, 0:1], scale=1.0 / H
+                out=own["squares"][:],
+                in_=own["u"][:],
+                func=ACT.Square,
+                bias=own["neg_mean"][:, 0:1],
+                scale=1.0,
+                accum_out=own["sum_sq"][:],
+            )
+            nc.scalar.activation(
+                out=own["rstd"][:],
+                in_=own["sum_sq"][:],
+                func=ACT.Abs_reciprocal_sqrt,
+                bias=eps_col[:, 0:1],
+                scale=1.0 / H,
             )
 
-        def center(t):
-            u, nmean, cen = st[t][0], st[t][2], st[t][7]
+        def centre(t):
+            own = tiles_of[t]
             nc.vector.scalar_tensor_tensor(
-                out=cen[:], in0=u[:], scalar=nmean[:, 0:1], in1=g_ps[:], op0=ALU.add, op1=ALU.mult
+                out=own["centred"][:],
+                in0=own["u"][:],
+                scalar=own["neg_mean"][:, 0:1],
+                in1=g_bank[:],
+                op0=ALU.add,
+                op1=ALU.mult,
             )
 
-        def recip(t):
-            return None
+        def scale_on_scalar(t, c0):
+            own = tiles_of[t]
+            scaled = work.tile([P, H - c0], F32, name="scaled%d" % t, tag="scaled")
+            nc.scalar.activation(out=scaled[:], in_=own["centred"][:, c0:H], func=ACT.Copy, scale=own["rstd"][:, 0:1])
+            return scaled
 
-        def scale_on_scalar(t, vc):
-            rstd, cen = st[t][5], st[t][7]
-            y = work.tile([P, H - vc], F32, name="y%d" % t, tag="y")
-            nc.scalar.activation(out=y[:], in_=cen[:, vc:H], func=ACT.Copy, scale=rstd[:, 0:1])
-            return y
-
-        def affine_v(t, c0, c1):
-            rstd, cen = st[t][5], st[t][7]
-            o_v = work.tile([P, c1 - c0], F32, name="ov%d_%d" % (t, c0), tag="ov")
+        def finish_on_vector(t, c0, c1):
+            own = tiles_of[t]
+            done = work.tile([P, c1 - c0], F32, name="done_v%d_%d" % (t, c0), tag="done_v")
             nc.vector.scalar_tensor_tensor(
-                out=o_v[:], in0=cen[:, c0:c1], scalar=rstd[:, 0:1], in1=b_ps[:, c0:c1], op0=ALU.mult, op1=ALU.add
+                out=done[:],
+                in0=own["centred"][:, c0:c1],
+                scalar=own["rstd"][:, 0:1],
+                in1=b_bank[:, c0:c1],
+                op0=ALU.mult,
+                op1=ALU.add,
             )
-            nc.sync.dma_start(out=outf[P * t : P * (t + 1), c0:c1], in_=o_v[:])
+            nc.sync.dma_start(out=out_rows[P * t : P * (t + 1), c0:c1], in_=done[:])
 
-        def affine_g(t, vc, y):
-            o_g = work.tile([P, H - vc], F32, name="og%d" % t, tag="og")
-            nc.gpsimd.tensor_tensor(out=o_g[:], in0=y[:], in1=b_sb[:, vc:H], op=ALU.add)
-            nc.sync.dma_start(out=outf[P * t : P * (t + 1), vc:H], in_=o_g[:])
+        def finish_on_gpsimd(t, c0, scaled):
+            done = work.tile([P, H - c0], F32, name="done_g%d" % t, tag="done_g")
+            nc.gpsimd.tensor_tensor(out=done[:], in0=scaled[:], in1=ln2_b_all[:, c0:H], op=ALU.add)
+            nc.sync.dma_start(out=out_rows[P * t : P * (t + 1), c0:H], in_=done[:])
 
-        LAST = NT - 1
-        for j in range(2 * NSPLIT):
-            t, r = units[j]
-            empty_part(t, r)
-            if r == 1:
-                preadd(nc.gpsimd, t)
-            run_unit(j + 3)
+        for m in range(N_PAIRS):
+            ride(m)
+        for m in range((len(RUNS) - 1) * N_RIDERS):
+            t, i = rides[m]
+            add_to_partial(t, i)
+            if i == len(RUNS) - 2:
+                make_addend(t)
+            ride(m + N_PAIRS)
+
         for t in range(LAST):
             begin(t)
-            add_piece(t, 0, 0, HALF)
+            empty_group(t, 0, 0, BANK)
             if t >= 1:
-                recip(t - 1)
-                y_prev = scale_on_scalar(t - 1, VC)
-            add_piece(t, 1, HALF, H)
-            stats_on_scalar(t, 2)
+                scaled = scale_on_scalar(t - 1, V_COLS)
+            empty_group(t, 1, BANK, H)
+            row_stats(t, 2)
             if t >= 1:
-                affine_v(t - 1, 0, VC)
-                affine_g(t - 1, VC, y_prev)
-                if t + 3 < NT:
-                    preadd(nc.gpsimd, t + 3)
-            center(t)
-            nxt = t + 3
-            if nxt == 3:
-                run_unit(3 * NSPLIT - 1)
-            elif nxt < LAST:
-                open_pair(nxt, (nxt + 2) % 3)
-                for h in range(2):
-                    for g in range(NPASS):
-                        mx(nxt, g, h)
-            if nxt == LAST:
-                open_bank(LAST, 0, 0)
-                for g in range(NPASS):
-                    mx(LAST, g, 0)
-                open_bank(LAST, 1, 1)
-                for g in range(NPASS):
-                    mx(LAST, g, 1, HALF, HALF + 256)
-            if nxt == LAST + 1:
-                open_bank(LAST, 2, 2)
-                for g in range(NPASS):
-                    mx(LAST, g, 2, HALF + 256, H)
+                finish_on_vector(t - 1, 0, V_COLS)
+                finish_on_gpsimd(t - 1, V_COLS, scaled)
+                if t + ADDEND_AHEAD < N_TILES:
+                    make_addend(t + ADDEND_AHEAD)
+            centre(t)
+            pair = ((len(RUNS) - 1) * N_RIDERS + t) % N_PAIRS
+            follower = t + N_PAIRS
+            if follower < N_RIDERS:
+                ride((len(RUNS) - 1) * N_RIDERS + follower)
+            elif follower < LAST:
+                whole_tile(follower, pair)
+            elif follower == LAST:
+                last_tile_piece(0, 2 * pair)
+                last_tile_piece(1, 2 * pair + 1)
+            elif follower == LAST + 1:
+                last_tile_piece(2, 2 * pair)
+
         begin(LAST)
-        add_piece(LAST, 0, 0, HALF)
-        recip(LAST - 1)
-        y_prev = scale_on_scalar(LAST - 1, VC)
-        add_piece(LAST, 1, HALF, HALF + 256)
-        affine_v(LAST - 1, 0, VC)
-        affine_g(LAST - 1, VC, y_prev)
-        add_piece(LAST, 2, HALF + 256, H)
-        stats_on_scalar(LAST, 3)
-        center(LAST)
-        recip(LAST)
-        y_prev = scale_on_scalar(LAST, VC_LAST)
-        affine_v(LAST, 0, VC_LAST // 2)
-        affine_g(LAST, VC_LAST, y_prev)
-        affine_v(LAST, VC_LAST // 2, VC_LAST)
+        empty_group(LAST, 0, LAST_PIECES[0][0], LAST_PIECES[0][1])
+        scaled = scale_on_scalar(LAST - 1, V_COLS)
+        empty_group(LAST, 1, LAST_PIECES[1][0], LAST_PIECES[1][1])
+        finish_on_vector(LAST - 1, 0, V_COLS)
+        finish_on_gpsimd(LAST - 1, V_COLS, scaled)
+        empty_group(LAST, 2, LAST_PIECES[2][0], LAST_PIECES[2][1])
+        row_stats(LAST, len(LAST_PIECES))
+        centre(LAST)
+        scaled = scale_on_scalar(LAST, V_COLS_LAST)
+        finish_on_vector(LAST, 0, V_COLS_LAST // 2)
+        finish_on_gpsimd(LAST, V_COLS_LAST, scaled)
+        finish_on_vector(LAST, V_COLS_LAST // 2, V_COLS_LAST)

@@ -84,10 +84,9 @@ def tile_disentangledattention_pc_kernel(
             for b, t in enumerate(tiles):
                 place_in_load[t] = (a, b)
 
-        ones = own_tile(const, [P, P], BF16, "ones")
-        vec_row = {}
-        for nm in ("b_f", "ln2_g", "ln2_b"):
-            vec_row[nm] = own_tile(const, [P, H], BF16, "row_%s" % nm)
+        vec_rows = own_tile(const, [P, H], BF16, "vec_rows")
+        pick = own_tile(const, [P, 3, P], BF16, "pick")
+        place_of = {"b_f": 0, "ln2_g": 1, "ln2_b": 2}
         b_f_all = own_tile(const, [P, H], BF16, "b_f_all")
         ln2_b_all = own_tile(const, [P, H], BF16, "ln2_b_all")
         eps_col = own_tile(const, [P, 1], F32, "eps_col")
@@ -104,12 +103,15 @@ def tile_disentangledattention_pc_kernel(
             addend.append(own_tile(keep, [P, H], F32, "addend%d" % t))
 
         nc.gpsimd.memset(zeros[:].bitcast(F32), 0.0)
-        nc.gpsimd.memset(rider_plane[0][:].bitcast(F32), 0.0)
-        nc.gpsimd.memset(w_plane[0][:].bitcast(F32), 0.0)
+        nc.vector.memset(rider_plane[0][:].bitcast(I32), 0)
+        nc.vector.memset(w_plane[0][:].bitcast(I32), 0)
+        nc.vector.memset(vec_rows[:].bitcast(I32), 0)
         for nm, vec in (("b_f", b_f), ("ln2_g", ln2_g), ("ln2_b", ln2_b)):
-            nc.vector.memset(vec_row[nm][:].bitcast(I32), 0)
-            nc.scalar.dma_start(out=vec_row[nm][0:1, :], in_=vec.unsqueeze(0))
-        nc.vector.memset(ones[:], 1.0)
+            j = place_of[nm]
+            nc.scalar.dma_start(out=vec_rows[QUADRANT * j : QUADRANT * j + 1, :], in_=vec.unsqueeze(0))
+        nc.vector.memset(pick[:].bitcast(I32), 0)
+        for j in range(3):
+            nc.vector.memset(pick[QUADRANT * j : QUADRANT * j + 1, j, :], 1.0)
         nc.vector.memset(eps_col[:], EPS)
         nc.scalar.activation(out=table_warm[:], in_=eps_col[:], func=ACT.Abs_reciprocal_sqrt)
         for i in range(1, len(RUNS)):
@@ -180,8 +182,8 @@ def tile_disentangledattention_pc_kernel(
             for h in range(2):
                 nc.tensor.matmul(
                     out=dst[:, BANK * h : BANK * (h + 1)],
-                    lhsT=ones[:],
-                    rhs=vec_row[nm][:, BANK * h : BANK * (h + 1)],
+                    lhsT=pick[:, place_of[nm], :],
+                    rhs=vec_rows[:, BANK * h : BANK * (h + 1)],
                     start=True,
                     stop=True,
                 )

from contextlib import ExitStack

import concourse.mybir as mybir

FLOPS = 2 * 1024 * 4096 * 1024

F32 = mybir.dt.float32
BF16 = mybir.dt.bfloat16
I32 = mybir.dt.int32
U8 = mybir.dt.uint8
FP4 = mybir.dt.float4_e2m1fn_x4
ALU = mybir.AluOpType
ACT = mybir.ActivationFunctionType

P = 128
QUADRANT = 32
ROWS_PER_QUADRANT = 4
SCALE_ROWS = 16
H = 1024
BANK = 512
N_PASS = 8
N_TILES = 8
LAST = N_TILES - 1
EPS = 1e-7

RUNS = ((0, 1), (2, 3, 4), (5, 6, 7))
N_RIDERS = 4
RIDER_TOKENS = P * N_RIDERS
LATE_TILES = ((4, 5), (6, 7))
N_PAIRS = 3

ADDEND_AHEAD = 3

V_COLS = 544
V_COLS_LAST = 896
LAST_PIECES = ((0, 512), (512, 768), (768, 1024))
N_WARM = 4


def tile_disentangledattention_pc_kernel(
    tc, ff_words, ff_scales, attn_out, Wf_words, Wf_scales, b_f, ln2_g, ln2_b, out
):
    nc = tc.nc
    attn = attn_out.flatten_outer_dims()
    out_rows = out.flatten_outer_dims()

    with ExitStack() as ctx:
        const = ctx.enter_context(tc.tile_pool(name="const", bufs=1))
        codes = ctx.enter_context(tc.tile_pool(name="codes", bufs=1))
        planes = ctx.enter_context(tc.tile_pool(name="planes", bufs=1))
        keep = ctx.enter_context(tc.tile_pool(name="keep", bufs=1))
        work = ctx.enter_context(tc.tile_pool(name="work", bufs=3))
        stats = ctx.enter_context(tc.tile_pool(name="stats", bufs=1))
        psum = ctx.enter_context(tc.psum_pool(name="psum", bufs=1))
        ctx.enter_context(tc.manual_schedule())

        def own_tile(pool, shape, dtype, name):
            return pool.tile(shape, dtype, name=name, tag=name)

        def operand_tile(pool, shape, name):
            return pool.tile(shape, U8, name=name, tag=name, align_bytes=64)

        w_plane = []
        rider_plane = []
        for i, run in enumerate(RUNS):
            w_plane.append(operand_tile(planes, [P, len(run), H], "w_plane%d" % i))
            rider_plane.append(operand_tile(planes, [P, len(run), RIDER_TOKENS], "rider_plane%d" % i))
        late_plane = operand_tile(planes, [P, N_PASS, H - RIDER_TOKENS], "late_plane")
        w_codes = []
        for g in range(N_PASS):
            w_codes.append(operand_tile(codes, [P, 2 * H], "w_codes%d" % g))
        rider_codes = []
        for i, run in enumerate(RUNS):
            rider_codes.append(operand_tile(codes, [P, len(run), 2 * RIDER_TOKENS], "rider_codes%d" % i))
        late_codes = []
        for a, tiles in enumerate(LATE_TILES):
            late_codes.append(operand_tile(codes, [P, N_PASS, 2 * P * len(tiles)], "late_codes%d" % a))
        place_in_run = {}
        for i, run in enumerate(RUNS):
            for j, g in enumerate(run):
                place_in_run[g] = (i, j)
        place_in_load = {}
        for a, tiles in enumerate(LATE_TILES):
            for b, t in enumerate(tiles):
                place_in_load[t] = (a, b)

        vec_rows = own_tile(const, [P, H], BF16, "vec_rows")
        pick = own_tile(const, [P, 3, P], BF16, "pick")
        place_of = {"b_f": 0, "ln2_g": 1, "ln2_b": 2}
        b_f_all = own_tile(const, [P, H], BF16, "b_f_all")
        ln2_b_all = own_tile(const, [P, H], BF16, "ln2_b_all")
        eps_col = own_tile(const, [P, 1], F32, "eps_col")
        table_warm = own_tile(const, [P, 1], F32, "table_warm")
        zeros = own_tile(const, [P, BANK], BF16, "zeros")
        g_bank = own_tile(psum, [P, H], BF16, "g_bank")
        b_bank = own_tile(psum, [P, H], BF16, "b_bank")

        attn_sb = []
        for t in range(N_TILES):
            attn_sb.append(own_tile(keep, [P, H], BF16, "attn%d" % t))
        addend = []
        for t in range(N_TILES):
            addend.append(own_tile(keep, [P, H], F32, "addend%d" % t))

        nc.gpsimd.memset(zeros[:].bitcast(F32), 0.0)
        nc.vector.memset(rider_plane[0][:].bitcast(I32), 0)
        nc.vector.memset(w_plane[0][:].bitcast(I32), 0)
        nc.vector.memset(vec_rows[:].bitcast(I32), 0)
        for nm, vec in (("b_f", b_f), ("ln2_g", ln2_g), ("ln2_b", ln2_b)):
            j = place_of[nm]
            nc.scalar.dma_start(out=vec_rows[QUADRANT * j : QUADRANT * j + 1, :], in_=vec.unsqueeze(0))
        nc.vector.memset(pick[:].bitcast(I32), 0)
        for j in range(3):
            nc.vector.memset(pick[QUADRANT * j : QUADRANT * j + 1, j, :], 1.0)
        nc.vector.memset(eps_col[:], EPS)
        nc.scalar.activation(out=table_warm[:], in_=eps_col[:], func=ACT.Abs_reciprocal_sqrt)
        for i in range(1, len(RUNS)):
            nc.vector.memset(w_plane[i][:].bitcast(I32), 0)
            nc.vector.memset(rider_plane[i][:].bitcast(I32), 0)
        nc.vector.memset(late_plane[:].bitcast(I32), 0)

        def load_scale_rows(plane, scales, g0, g1, n0, n1):
            for r in range(ROWS_PER_QUADRANT):
                nc.sync.dma_start(
                    out=plane[r:P:QUADRANT, :, :].bitcast(I32),
                    in_=scales[g0:g1, r:SCALE_ROWS:ROWS_PER_QUADRANT, n0:n1].rearrange("g q n -> q g n").bitcast(I32),
                )

        def load_run_scales(i):
            g0 = RUNS[i][0]
            g1 = RUNS[i][-1] + 1
            load_scale_rows(rider_plane[i], ff_scales, g0, g1, 0, RIDER_TOKENS)
            load_scale_rows(w_plane[i], Wf_scales, g0, g1, 0, H)

        def load_w_codes(g):
            nc.sync.dma_start(out=w_codes[g][:].bitcast(I32), in_=Wf_words[g].bitcast(I32))

        def load_rider_codes(i):
            g0 = RUNS[i][0]
            g1 = RUNS[i][-1] + 1
            nc.sync.dma_start(
                out=rider_codes[i][:].bitcast(I32),
                in_=ff_words[g0:g1, :, 0 : 2 * RIDER_TOKENS].rearrange("g p n -> p g n").bitcast(I32),
            )

        def load_late_codes(a):
            t0 = LATE_TILES[a][0]
            t1 = LATE_TILES[a][-1] + 1
            nc.sync.dma_start(
                out=late_codes[a][:].bitcast(I32),
                in_=ff_words[:, :, 2 * P * t0 : 2 * P * t1].rearrange("g p n -> p g n").bitcast(I32),
            )

        def load_attn(t):
            nc.sync.dma_start(out=attn_sb[t][:], in_=attn[P * t : P * (t + 1), :])

        load_w_codes(0)
        load_rider_codes(0)
        load_run_scales(0)
        load_w_codes(1)
        load_w_codes(2)
        load_rider_codes(1)
        load_run_scales(1)
        load_w_codes(3)
        load_w_codes(4)
        load_attn(0)
        load_w_codes(5)
        load_rider_codes(2)
        load_run_scales(2)
        load_attn(1)
        load_w_codes(6)
        load_w_codes(7)
        load_attn(2)
        load_attn(3)
        load_scale_rows(late_plane, ff_scales, 0, N_PASS, RIDER_TOKENS, H)
        load_late_codes(0)
        load_late_codes(1)
        for t in range(N_RIDERS, N_TILES):
            load_attn(t)

        def spread(nm, dst):
            for h in range(2):
                nc.tensor.matmul(
                    out=dst[:, BANK * h : BANK * (h + 1)],
                    lhsT=pick[:, place_of[nm], :],
                    rhs=vec_rows[:, BANK * h : BANK * (h + 1)],
                    start=True,
                    stop=True,
                )

        warm_bank = psum.tile([P, BANK], F32, name="warm_bank", tag="bank0")
        for rep in range(N_WARM):
            nc.tensor.matmul(out=warm_bank[:], lhsT=zeros[:, 0:P], rhs=zeros[:], start=True, stop=True)
        b_f_bank = psum.tile([P, H], BF16, name="b_f_bank", tag="bank5")
        spread("b_f", b_f_bank)
        nc.scalar.copy(out=b_f_all[:], in_=b_f_bank[:])
        spread("ln2_g", g_bank)
        spread("ln2_b", b_bank)
        nc.scalar.copy(out=ln2_b_all[:], in_=b_bank[:])

        group = {}

        def open_group(t, piece, bank):
            group[(t, piece)] = psum.tile(
                [P, BANK], F32, name="group%d_%d_bank%d" % (t, piece, bank), tag="bank%d" % bank
            )

        def open_pair(t, pair):
            for h in range(2):
                open_group(t, h, 2 * pair + h)

        def multiply(t, g, piece, c0, c1, first, last):
            i, j = place_in_run[g]
            if t < N_RIDERS:
                tokens = rider_codes[i][:, j, 2 * P * t : 2 * P * (t + 1)]
                token_scales = rider_plane[i][:, j, P * t : P * (t + 1)]
            else:
                a, b = place_in_load[t]
                tokens = late_codes[a][:, g, 2 * P * b : 2 * P * (b + 1)]
                token_scales = late_plane[:, g, P * t - RIDER_TOKENS : P * (t + 1) - RIDER_TOKENS]
            nc.tensor.matmul_mx(
                out=group[(t, piece)][:, 0 : c1 - c0],
                lhsT=tokens.bitcast(FP4),
                lhsT_scale=token_scales,
                rhs=w_codes[g][:, 2 * c0 : 2 * c1].bitcast(FP4),
                rhs_scale=w_plane[i][:, j, c0:c1],
                start=(g == first),
                stop=(g == last),
            )

        rides = []
        for i in range(len(RUNS)):
            for t in range(N_RIDERS):
                rides.append((t, i))

        def ride(m):
            t, i = rides[m]
            open_pair(t, m % N_PAIRS)
            for g in RUNS[i]:
                for h in range(2):
                    multiply(t, g, h, BANK * h, BANK * (h + 1), RUNS[i][0], RUNS[i][-1])

        def whole_tile(t, pair):
            open_pair(t, pair)
            for h in range(2):
                for g in range(N_PASS):
                    multiply(t, g, h, BANK * h, BANK * (h + 1), 0, N_PASS - 1)

        def last_tile_piece(piece, bank):
            c0, c1 = LAST_PIECES[piece]
            open_group(LAST, piece, bank)
            for g in range(N_PASS):
                multiply(LAST, g, piece, c0, c1, 0, N_PASS - 1)

        partial = {}

        def add_to_partial(t, i):
            so_far = b_f_all if i == 0 else partial[t]
            partial[t] = own_tile(keep, [P, H], F32, "partial%d_%d" % (t, i))
            for h in range(2):
                nc.vector.tensor_tensor(
                    out=partial[t][:, BANK * h : BANK * (h + 1)],
                    in0=group[(t, h)][:],
                    in1=so_far[:, BANK * h : BANK * (h + 1)],
                    op=ALU.add,
                )

        def make_addend(t):
            rest = partial[t] if t < N_RIDERS else b_f_all
            nc.gpsimd.tensor_tensor(out=addend[t][:], in0=attn_sb[t][:], in1=rest[:], op=ALU.add)

        tiles_of = {}

        def begin(t):
            tiles_of[t] = {
                "u": work.tile([P, H], F32, name="u%d" % t, tag="u"),
                "row_sums": own_tile(stats, [P, len(LAST_PIECES)], F32, "row_sums%d" % t),
                "scaled_sums": own_tile(stats, [P, len(LAST_PIECES)], F32, "scaled_sums%d" % t),
                "neg_mean": own_tile(stats, [P, 1], F32, "neg_mean%d" % t),
                "sum_sq": own_tile(stats, [P, 1], F32, "sum_sq%d" % t),
                "rstd": own_tile(stats, [P, 1], F32, "rstd%d" % t),
                "squares": work.tile([P, H], BF16, name="squares%d" % t, tag="squares"),
                "centred": work.tile([P, H], F32, name="centred%d" % t, tag="centred"),
            }

        def empty_group(t, piece, c0, c1):
            own = tiles_of[t]
            nc.vector.scalar_tensor_tensor(
                out=own["u"][:, c0:c1],
                in0=group[(t, piece)][:, 0 : c1 - c0],
                scalar=1.0,
                in1=addend[t][:, c0:c1],
                op0=ALU.mult,
                op1=ALU.add,
                accum_out=own["row_sums"][:, piece : piece + 1],
            )

        def row_stats(t, n_pieces):
            own = tiles_of[t]
            nc.scalar.activation(
                out=own["scaled_sums"][:, 0:n_pieces],
                in_=own["row_sums"][:, 0:n_pieces],
                func=ACT.Copy,
                scale=-1.0 / H,
                accum_out=own["neg_mean"][:],
            )
            nc.scalar.activation(
                out=own["squares"][:],
                in_=own["u"][:],
                func=ACT.Square,
                bias=own["neg_mean"][:, 0:1],
                scale=1.0,
                accum_out=own["sum_sq"][:],
            )
            nc.scalar.activation(
                out=own["rstd"][:],
                in_=own["sum_sq"][:],
                func=ACT.Abs_reciprocal_sqrt,
                bias=eps_col[:, 0:1],
                scale=1.0 / H,
            )

        def centre(t):
            own = tiles_of[t]
            nc.vector.scalar_tensor_tensor(
                out=own["centred"][:],
                in0=own["u"][:],
                scalar=own["neg_mean"][:, 0:1],
                in1=g_bank[:],
                op0=ALU.add,
                op1=ALU.mult,
            )

        def scale_on_scalar(t, c0):
            own = tiles_of[t]
            scaled = work.tile([P, H - c0], F32, name="scaled%d" % t, tag="scaled")
            nc.scalar.activation(out=scaled[:], in_=own["centred"][:, c0:H], func=ACT.Copy, scale=own["rstd"][:, 0:1])
            return scaled

        def finish_on_vector(t, c0, c1):
            own = tiles_of[t]
            done = work.tile([P, c1 - c0], F32, name="done_v%d_%d" % (t, c0), tag="done_v")
            nc.vector.scalar_tensor_tensor(
                out=done[:],
                in0=own["centred"][:, c0:c1],
                scalar=own["rstd"][:, 0:1],
                in1=b_bank[:, c0:c1],
                op0=ALU.mult,
                op1=ALU.add,
            )
            nc.sync.dma_start(out=out_rows[P * t : P * (t + 1), c0:c1], in_=done[:])

        def finish_on_gpsimd(t, c0, scaled):
            done = work.tile([P, H - c0], F32, name="done_g%d" % t, tag="done_g")
            nc.gpsimd.tensor_tensor(out=done[:], in0=scaled[:], in1=ln2_b_all[:, c0:H], op=ALU.add)
            nc.sync.dma_start(out=out_rows[P * t : P * (t + 1), c0:H], in_=done[:])

        for m in range(N_PAIRS):
            ride(m)
        for m in range((len(RUNS) - 1) * N_RIDERS):
            t, i = rides[m]
            add_to_partial(t, i)
            if i == len(RUNS) - 2:
                make_addend(t)
            ride(m + N_PAIRS)

        for t in range(LAST):
            begin(t)
            empty_group(t, 0, 0, BANK)
            if t >= 1:
                scaled = scale_on_scalar(t - 1, V_COLS)
            empty_group(t, 1, BANK, H)
            row_stats(t, 2)
            if t >= 1:
                finish_on_vector(t - 1, 0, V_COLS)
                finish_on_gpsimd(t - 1, V_COLS, scaled)
                if t + ADDEND_AHEAD < N_TILES:
                    make_addend(t + ADDEND_AHEAD)
            centre(t)
            pair = ((len(RUNS) - 1) * N_RIDERS + t) % N_PAIRS
            follower = t + N_PAIRS
            if follower < N_RIDERS:
                ride((len(RUNS) - 1) * N_RIDERS + follower)
            elif follower < LAST:
                whole_tile(follower, pair)
            elif follower == LAST:
                last_tile_piece(0, 2 * pair)
                last_tile_piece(1, 2 * pair + 1)
            elif follower == LAST + 1:
                last_tile_piece(2, 2 * pair)

        begin(LAST)
        empty_group(LAST, 0, LAST_PIECES[0][0], LAST_PIECES[0][1])
        scaled = scale_on_scalar(LAST - 1, V_COLS)
        empty_group(LAST, 1, LAST_PIECES[1][0], LAST_PIECES[1][1])
        finish_on_vector(LAST - 1, 0, V_COLS)
        finish_on_gpsimd(LAST - 1, V_COLS, scaled)
        empty_group(LAST, 2, LAST_PIECES[2][0], LAST_PIECES[2][1])
        row_stats(LAST, len(LAST_PIECES))
        centre(LAST)
        scaled = scale_on_scalar(LAST, V_COLS_LAST)
        finish_on_vector(LAST, 0, V_COLS_LAST // 2)
        finish_on_gpsimd(LAST, V_COLS_LAST, scaled)
        finish_on_vector(LAST, V_COLS_LAST // 2, V_COLS_LAST)
